import numpy as np
import ml_dtypes


def mxq(x, axis, fmt="e4m3"):
    dtype, down = {"e4m3": (ml_dtypes.float8_e4m3fn, 7), "e5m2": (ml_dtypes.float8_e5m2, 14)}[fmt]
    v = np.moveaxis(np.asarray(x, np.float32).astype(ml_dtypes.bfloat16).astype(np.float64), axis, -1)
    blocks = v.reshape(v.shape[:-1] + (-1, 32))
    amax = np.abs(blocks).max(-1, keepdims=True)
    byte = np.maximum(np.where(amax > 0, np.frexp(amax)[1] - 1 + 127, 0) - down, 1)
    scale = np.exp2(byte - 127.0)
    codes = (blocks / scale).astype(np.float32).astype(dtype).astype(np.float64)
    return np.moveaxis((codes * scale).reshape(v.shape), -1, axis)


WIDE = False


def mx_kscale(k):
    if not WIDE:
        return np.ones(k)
    levels = np.array([10, -10, 5, -5, 0])
    a = np.random.permutation(np.resize(levels, k // 512 * 4)).reshape(k // 512, 4)
    idx = np.arange(k)
    return np.exp2(a[idx // 512, idx % 128 // 32])


BF16 = ml_dtypes.bfloat16


def bf(x):
    return np.asarray(x, np.float32).astype(BF16)


def f64(x):
    return np.asarray(x).astype(np.float64)


B, S, D, E, F, NH, BAND = 4, 256, 512, 512, 1024, 4, 6
HG = E // NH
EPS = 1e-5
ZCAP = 5.9


def layernorm(x, w, b):
    m = x.mean(-1, keepdims=True)
    v = ((x - m) ** 2).mean(-1, keepdims=True)
    return (x - m) / np.sqrt(v + EPS) * w + b


def erf(z):
    a = np.minimum(np.abs(z), ZCAP)
    term = a.copy()
    tot = a.copy()
    for n in np.arange(1.0, 3.0 * ZCAP * ZCAP):
        term = term * (2.0 * a * a / (2.0 * n + 1.0))
        tot = tot + term
    return np.sign(z) * 2.0 / np.sqrt(np.pi) * np.exp(-a * a) * tot


def gelu_erf(u):
    return 0.5 * u * (1.0 + erf(u / np.sqrt(2.0)))


def setup_inputs():
    r = np.random.standard_normal
    s = mx_kscale(E)
    return {
        "o_glob": bf(r((B, NH, S, HG)) * 0.35 * s.reshape(NH, 1, HG)),
        "x_loc": bf(r((B, S, D)) * 1.1),
        "Wo_g": bf(r((D, E)) * 2.0 / np.sqrt(E) / s),
        "bo_g": bf(r(D) * 0.1),
        "ln3_w": bf(1.0 + 0.1 * r(D)),
        "ln3_b": bf(r(D) * 0.1),
        "W1": bf(r((F, D)) / np.sqrt(D)),
        "b1": bf(r(F) * 0.2),
    }


def reference(o_glob, x_loc, Wo_g, bo_g, ln3_w, ln3_b, W1, b1):
    o = f64(o_glob).transpose(0, 2, 1, 3).reshape(B, S, E)
    x_glob = f64(x_loc) + ((mxq(o, 2, "e4m3") @ mxq(f64(Wo_g), 1, "e4m3").T) + f64(bo_g))
    h = layernorm(x_glob, f64(ln3_w), f64(ln3_b))
    u = (mxq(h, 2, "e4m3") @ mxq(f64(W1), 1, "e4m3").T) + f64(b1)
    return x_glob, gelu_erf(u)

@@ -1,0 +1,245 @@
+import concourse.mybir as mybir
+from concourse.masks import make_identity
+
+F32 = mybir.dt.float32
+BF16 = mybir.dt.bfloat16
+U32 = mybir.dt.uint32
+U8 = mybir.dt.uint8
+FP8X4 = mybir.dt.float8_e4m3fn_x4
+ALU = mybir.AluOpType
+ACT = mybir.ActivationFunctionType
+
+P = 128
+PACK = 4
+K = P * PACK
+WORDS = K // 2
+TOKENS = 1024
+TILES = TOKENS // P
+D = 512
+F = 1024
+BANK = 512
+EPS = 1e-5
+
+FLOPS = 2 * TOKENS * K * D + 2 * TOKENS * K * F
+
+
+def two_blocks_k_onto_partitions(nc, banks, identity, rows, grouped, block):
+    bank = banks.tile([P, 2, 2, P], F32, tag="bank")
+    for j in range(2):
+        pairs = rows[:, block + j, :].rearrange("r (p u) -> r p u", u=2)
+        for u in range(2):
+            nc.tensor.transpose(bank[:, j, u, :], pairs[:, :, u], identity[:])
+    nc.scalar.copy(
+        out=grouped[:, block * P : (block + 2) * P, :].rearrange("p (j r) u -> p j r u", j=2),
+        in_=bank[:].rearrange("p j u r -> p j r u"),
+    )
+
+
+def quantise_rows(nc, grouped, codes, scales, first, count):
+    nc.vector.quantize_mx(
+        out=codes[:, first : first + count].bitcast(FP8X4),
+        scales=scales[:, first : first + count],
+        in_=grouped[:, first : first + count, :].rearrange("p r t -> p (r t)"),
+    )
+
+
+def tile_block_pb_kernel(
+    tc, o_glob, x_loc, Wo_g, bo_g, ln3_w, ln3_b, W1, b1, out_0, out_1
+):
+    nc = tc.nc
+    x_glob_out = out_0.flatten_outer_dims()
+    g_out = out_1.flatten_outer_dims()
+
+    with tc.tile_pool(name="keep", bufs=1) as keep, tc.tile_pool(
+        name="work", bufs=3
+    ) as work, tc.tile_pool(name="stats", bufs=4) as stats, tc.psum_pool(
+        name="banks", bufs=2
+    ) as banks, tc.psum_pool(name="acc_one", bufs=2) as acc_one, tc.psum_pool(
+        name="acc_two", bufs=4
+    ) as acc_two:
+        wo_rows = keep.tile([P, D // P, K], BF16)
+        o_rows = keep.tile([P, TILES, K], BF16)
+        x_rows = keep.tile([P, TILES, D], BF16)
+        w1_rows = keep.tile([P, F // P, K], BF16)
+        bo_all = keep.tile([P, D], BF16)
+        b1_all = keep.tile([P, F], BF16)
+        ln_w_bf = keep.tile([P, PACK], BF16)
+        ln_b_bf = keep.tile([P, PACK], BF16)
+
+        o_tiles = o_glob.rearrange("b n (h s) d -> b h s n d", s=P)
+        x_tiles = x_loc.flatten_outer_dims().rearrange("(i r) d -> r i d", r=P)
+        w1_blocks = W1.rearrange("(c r) k -> r c k", r=P)
+        half_tiles = TILES // 2
+
+        def load_o(i):
+            nc.sync.dma_start(
+                out=o_rows[:, i, :].rearrange("s (n d) -> s n d", d=P), in_=o_tiles[i // 2, i % 2]
+            )
+
+        nc.sync.dma_start(out=wo_rows[:], in_=Wo_g.rearrange("(c r) k -> r c k", r=P))
+        load_o(0)
+        load_o(1)
+        nc.sync.dma_start(out=bo_all[:], in_=bo_g.partition_broadcast(P))
+        nc.sync.dma_start(out=x_rows[:, :half_tiles, :], in_=x_tiles[:, :half_tiles, :])
+        for i in range(2, TILES):
+            load_o(i)
+        nc.sync.dma_start(out=w1_rows[:, :4, :], in_=w1_blocks[:, :4, :])
+        nc.sync.dma_start(out=w1_rows[:, 4:, :], in_=w1_blocks[:, 4:, :])
+        nc.sync.dma_start(out=ln_w_bf[:], in_=ln3_w.rearrange("(p t) -> p t", t=PACK))
+        nc.sync.dma_start(out=ln_b_bf[:], in_=ln3_b.rearrange("(p t) -> p t", t=PACK))
+        nc.sync.dma_start(out=b1_all[:], in_=b1.partition_broadcast(P))
+        nc.sync.dma_start(out=x_rows[:, half_tiles:, :], in_=x_tiles[:, half_tiles:, :])
+
+        identity = keep.tile([P, P], F32)
+        make_identity(nc, identity[:])
+        minus_half = keep.tile([P, 1], F32)
+        nc.vector.memset(minus_half[:], -0.5)
+        table_in = keep.tile([P, 1], F32)
+        table_out = keep.tile([P, 1], F32)
+        nc.vector.memset(table_in[:], 0.0)
+        nc.scalar.activation(out=table_out[:], in_=table_in[:], func=ACT.Gelu)
+        ln_w = keep.tile([P, PACK], F32)
+        ln_b = keep.tile([P, PACK], F32)
+        nc.vector.tensor_copy(out=ln_w[:], in_=ln_w_bf[:])
+        nc.vector.tensor_copy(out=ln_b[:], in_=ln_b_bf[:])
+
+        wo_grouped = keep.tile([P, D, PACK], BF16, align_bytes=64)
+        wo_codes = keep.tile([P, D], U32, align_bytes=64)
+        wo_scales = keep.tile([P, D], U8, align_bytes=64)
+        o_grouped = keep.tile([P, TOKENS, PACK], BF16, align_bytes=64)
+        o_codes = keep.tile([P, TOKENS], U32, align_bytes=64)
+        o_scales = keep.tile([P, TOKENS], U8, align_bytes=64)
+        w1_grouped = keep.tile([P, F, PACK], BF16, align_bytes=64)
+        w1_codes = keep.tile([P, F], U32, align_bytes=64)
+        w1_scales = keep.tile([P, F], U8, align_bytes=64)
+
+        for block in range(0, D // P, 2):
+            two_blocks_k_onto_partitions(
+                nc, banks, identity, wo_rows[:].bitcast(F32), wo_grouped[:].bitcast(F32), block
+            )
+        quantise_rows(nc, wo_grouped, wo_codes, wo_scales, 0, D)
+        for block in range(0, TILES, 2):
+            two_blocks_k_onto_partitions(
+                nc, banks, identity, o_rows[:].bitcast(F32), o_grouped[:].bitcast(F32), block
+            )
+            quantise_rows(nc, o_grouped, o_codes, o_scales, block * P, 2 * P)
+        for block in range(0, F // P, 2):
+            two_blocks_k_onto_partitions(
+                nc, banks, identity, w1_rows[:].bitcast(F32), w1_grouped[:].bitcast(F32), block
+            )
+        for first in range(0, F, BANK):
+            quantise_rows(nc, w1_grouped, w1_codes, w1_scales, first, BANK)
+
+        for i in range(TILES):
+            tokens = slice(i * P, (i + 1) * P)
+
+            residual = work.tile([P, D], F32, bufs=TILES)
+            nc.gpsimd.tensor_tensor(
+                out=residual[:], in0=x_rows[:, i, :], in1=bo_all[:], op=ALU.add
+            )
+
+            product = acc_one.tile([P, D], F32)
+            nc.tensor.matmul_mx(
+                out=product[:],
+                lhsT=o_codes[:, tokens].bitcast(FP8X4),
+                lhsT_scale=o_scales[:, tokens],
+                rhs=wo_codes[:].bitcast(FP8X4),
+                rhs_scale=wo_scales[:],
+                start=True,
+                stop=True,
+            )
+            x_glob = work.tile([P, D], F32)
+            row_sum = stats.tile([P, 1], F32)
+            nc.vector.scalar_tensor_tensor(
+                out=x_glob[:],
+                in0=product[:],
+                scalar=0.0,
+                in1=residual[:],
+                op0=ALU.add,
+                op1=ALU.add,
+                accum_out=row_sum[:],
+            )
+            nc.sync.dma_start(out=x_glob_out[tokens, :], in_=x_glob[:])
+
+            minus_mean = stats.tile([P, 1], F32)
+            nc.gpsimd.tensor_scalar(
+                out=minus_mean[:],
+                in0=row_sum[:],
+                scalar1=-1.0 / D,
+                scalar2=0.0,
+                op0=ALU.mult,
+                op1=ALU.add,
+            )
+            squares = work.tile([P, D], BF16)
+            square_sum = stats.tile([P, 1], F32)
+            nc.scalar.activation(
+                out=squares[:],
+                in_=x_glob[:],
+                func=ACT.Square,
+                bias=minus_mean[:],
+                scale=1.0,
+                accum_out=square_sum[:],
+            )
+            var_eps = stats.tile([P, 1], F32)
+            nc.gpsimd.tensor_scalar(
+                out=var_eps[:],
+                in0=square_sum[:],
+                scalar1=1.0 / D,
+                scalar2=EPS,
+                op0=ALU.mult,
+                op1=ALU.add,
+            )
+            inv_std = stats.tile([P, 1], F32)
+            nc.gpsimd.tensor_tensor(
+                out=inv_std[:], in0=var_eps[:], in1=minus_half[:], op=ALU.pow
+            )
+
+            centred = work.tile([P, PACK, P], F32)
+            nc.vector.tensor_scalar(
+                out=centred[:],
+                in0=x_glob[:].rearrange("r (p t) -> r t p", t=PACK),
+                scalar1=minus_mean[:],
+                scalar2=inv_std[:],
+                op0=ALU.add,
+                op1=ALU.mult,
+            )
+            centred_t = banks.tile([P, PACK, P], F32, tag="bank")
+            for t in range(PACK):
+                nc.tensor.transpose(centred_t[:, t, :], centred[:, t, :], identity[:])
+            h_planes = work.tile([P, PACK, P], BF16)
+            for t in range(PACK):
+                nc.scalar.activation(
+                    out=h_planes[:, t, :],
+                    in_=centred_t[:, t, :],
+                    func=ACT.Identity,
+                    scale=ln_w[:, t : t + 1],
+                    bias=ln_b[:, t : t + 1],
+                )
+            h_grouped = work.tile([P, P, PACK], BF16, align_bytes=64)
+            nc.vector.tensor_copy(
+                out=h_grouped[:].rearrange("p (c i) t -> p c t i", i=4),
+                in_=h_planes[:].rearrange("p t (c i) -> p c t i", i=4),
+            )
+            h_codes = work.tile([P, P], U32, align_bytes=64)
+            h_scales = work.tile([P, P], U8, align_bytes=64)
+            quantise_rows(nc, h_grouped, h_codes, h_scales, 0, P)
+
+            g_tile = work.tile([P, F], F32)
+            for first in range(0, F, BANK):
+                features = slice(first, first + BANK)
+                up = acc_two.tile([P, BANK], F32)
+                nc.tensor.matmul_mx(
+                    out=up[:],
+                    lhsT=h_codes[:].bitcast(FP8X4),
+                    lhsT_scale=h_scales[:],
+                    rhs=w1_codes[:, features].bitcast(FP8X4),
+                    rhs_scale=w1_scales[:, features],
+                    start=True,
+                    stop=True,
+                )
+                biased = work.tile([P, BANK], F32, bufs=4)
+                nc.vector.tensor_tensor(
+                    out=biased[:], in0=up[:], in1=b1_all[:, features], op=ALU.add
+                )
+                nc.scalar.activation(out=g_tile[:, features], in_=biased[:], func=ACT.Gelu)
+            nc.sync.dma_start(out=g_out[tokens, :], in_=g_tile[:])

@@ -1,3 +1,5 @@
+from contextlib import ExitStack
+
 import concourse.mybir as mybir
 from concourse.masks import make_identity
 
@@ -12,24 +14,24 @@ ACT = mybir.ActivationFunctionType
 P = 128
 PACK = 4
 K = P * PACK
-WORDS = K // 2
 TOKENS = 1024
 TILES = TOKENS // P
 D = 512
 F = 1024
 BANK = 512
 EPS = 1e-5
+LAST_LAG = 6
 
 FLOPS = 2 * TOKENS * K * D + 2 * TOKENS * K * F
 
 
-def two_blocks_k_onto_partitions(nc, banks, identity, rows, grouped, block):
-    bank = banks.tile([P, 2, 2, P], F32, tag="bank")
+def flip_two_blocks(nc, psum, identity, rows, grouped, block, copy):
+    bank = psum.tile([P, 2, 2, P], F32, tag="bank", bufs=3)
     for j in range(2):
         pairs = rows[:, block + j, :].rearrange("r (p u) -> r p u", u=2)
         for u in range(2):
             nc.tensor.transpose(bank[:, j, u, :], pairs[:, :, u], identity[:])
-    nc.scalar.copy(
+    copy(
         out=grouped[:, block * P : (block + 2) * P, :].rearrange("p (j r) u -> p j r u", j=2),
         in_=bank[:].rearrange("p j u r -> p j r u"),
     )
@@ -50,58 +52,25 @@ def tile_block_pb_kernel(
     x_glob_out = out_0.flatten_outer_dims()
     g_out = out_1.flatten_outer_dims()
 
-    with tc.tile_pool(name="keep", bufs=1) as keep, tc.tile_pool(
-        name="work", bufs=3
-    ) as work, tc.tile_pool(name="stats", bufs=4) as stats, tc.psum_pool(
-        name="banks", bufs=2
-    ) as banks, tc.psum_pool(name="acc_one", bufs=2) as acc_one, tc.psum_pool(
-        name="acc_two", bufs=4
-    ) as acc_two:
+    with ExitStack() as stack:
+        keep = stack.enter_context(tc.tile_pool(name="keep", bufs=1))
+        psum = stack.enter_context(tc.psum_pool(name="psum", bufs=2))
+
         wo_rows = keep.tile([P, D // P, K], BF16)
         o_rows = keep.tile([P, TILES, K], BF16)
         x_rows = keep.tile([P, TILES, D], BF16)
         w1_rows = keep.tile([P, F // P, K], BF16)
-        bo_all = keep.tile([P, D], BF16)
-        b1_all = keep.tile([P, F], BF16)
         ln_w_bf = keep.tile([P, PACK], BF16)
         ln_b_bf = keep.tile([P, PACK], BF16)
-
-        o_tiles = o_glob.rearrange("b n (h s) d -> b h s n d", s=P)
-        x_tiles = x_loc.flatten_outer_dims().rearrange("(i r) d -> r i d", r=P)
-        w1_blocks = W1.rearrange("(c r) k -> r c k", r=P)
-        half_tiles = TILES // 2
-
-        def load_o(i):
-            nc.sync.dma_start(
-                out=o_rows[:, i, :].rearrange("s (n d) -> s n d", d=P), in_=o_tiles[i // 2, i % 2]
-            )
-
-        nc.sync.dma_start(out=wo_rows[:], in_=Wo_g.rearrange("(c r) k -> r c k", r=P))
-        load_o(0)
-        load_o(1)
-        nc.sync.dma_start(out=bo_all[:], in_=bo_g.partition_broadcast(P))
-        nc.sync.dma_start(out=x_rows[:, :half_tiles, :], in_=x_tiles[:, :half_tiles, :])
-        for i in range(2, TILES):
-            load_o(i)
-        nc.sync.dma_start(out=w1_rows[:, :4, :], in_=w1_blocks[:, :4, :])
-        nc.sync.dma_start(out=w1_rows[:, 4:, :], in_=w1_blocks[:, 4:, :])
-        nc.sync.dma_start(out=ln_w_bf[:], in_=ln3_w.rearrange("(p t) -> p t", t=PACK))
-        nc.sync.dma_start(out=ln_b_bf[:], in_=ln3_b.rearrange("(p t) -> p t", t=PACK))
-        nc.sync.dma_start(out=b1_all[:], in_=b1.partition_broadcast(P))
-        nc.sync.dma_start(out=x_rows[:, half_tiles:, :], in_=x_tiles[:, half_tiles:, :])
-
-        identity = keep.tile([P, P], F32)
-        make_identity(nc, identity[:])
-        minus_half = keep.tile([P, 1], F32)
-        nc.vector.memset(minus_half[:], -0.5)
-        table_in = keep.tile([P, 1], F32)
-        table_out = keep.tile([P, 1], F32)
-        nc.vector.memset(table_in[:], 0.0)
-        nc.scalar.activation(out=table_out[:], in_=table_in[:], func=ACT.Gelu)
         ln_w = keep.tile([P, PACK], F32)
         ln_b = keep.tile([P, PACK], F32)
-        nc.vector.tensor_copy(out=ln_w[:], in_=ln_w_bf[:])
-        nc.vector.tensor_copy(out=ln_b[:], in_=ln_b_bf[:])
+        bias_rows = keep.tile([P, D + F], BF16)
+        bias_all = keep.tile([P, D + F], BF16)
+        ones = keep.tile([P, P], BF16)
+        identity = keep.tile([P, P], F32)
+        minus_half = keep.tile([P, 1], F32)
+        table_in = keep.tile([P, 1], F32)
+        table_out = keep.tile([P, 1], F32)
 
         wo_grouped = keep.tile([P, D, PACK], BF16, align_bytes=64)
         wo_codes = keep.tile([P, D], U32, align_bytes=64)
@@ -112,134 +81,236 @@ def tile_block_pb_kernel(
         w1_grouped = keep.tile([P, F, PACK], BF16, align_bytes=64)
         w1_codes = keep.tile([P, F], U32, align_bytes=64)
         w1_scales = keep.tile([P, F], U8, align_bytes=64)
+        h_grouped = keep.tile([P, TOKENS, PACK], BF16, align_bytes=64)
+        h_codes = keep.tile([P, TOKENS], U32, align_bytes=64)
+        h_scales = keep.tile([P, TOKENS], U8, align_bytes=64)
 
-        for block in range(0, D // P, 2):
-            two_blocks_k_onto_partitions(
-                nc, banks, identity, wo_rows[:].bitcast(F32), wo_grouped[:].bitcast(F32), block
-            )
-        quantise_rows(nc, wo_grouped, wo_codes, wo_scales, 0, D)
-        for block in range(0, TILES, 2):
-            two_blocks_k_onto_partitions(
-                nc, banks, identity, o_rows[:].bitcast(F32), o_grouped[:].bitcast(F32), block
-            )
-            quantise_rows(nc, o_grouped, o_codes, o_scales, block * P, 2 * P)
-        for block in range(0, F // P, 2):
-            two_blocks_k_onto_partitions(
-                nc, banks, identity, w1_rows[:].bitcast(F32), w1_grouped[:].bitcast(F32), block
-            )
-        for first in range(0, F, BANK):
-            quantise_rows(nc, w1_grouped, w1_codes, w1_scales, first, BANK)
+        x_glob = keep.tile([P, TILES, D], F32)
+        squares = keep.tile([P, TILES, D], BF16)
+        centred = keep.tile([P, TILES, PACK, P], F32)
+        h_planes = keep.tile([P, TILES, PACK, P], BF16)
+        g = keep.tile([P, TILES, F], F32)
+        row_sum = keep.tile([P, TILES], F32)
+        minus_mean = keep.tile([P, TILES], F32)
+        square_sum = keep.tile([P, TILES], F32)
+        var_eps = keep.tile([P, TILES], F32)
+        inv_std = keep.tile([P, TILES], F32)
 
-        for i in range(TILES):
-            tokens = slice(i * P, (i + 1) * P)
+        products = {}
+        flipped = {}
+        ups = {}
 
-            residual = work.tile([P, D], F32, bufs=TILES)
-            nc.gpsimd.tensor_tensor(
-                out=residual[:], in0=x_rows[:, i, :], in1=bo_all[:], op=ALU.add
+        nc.vector.memset(bias_rows[:], 0.0)
+        nc.vector.memset(ones[:], 1.0)
+        nc.vector.memset(minus_half[:], -0.5)
+        nc.vector.memset(table_in[:], 0.0)
+        make_identity(nc, identity[:])
+        nc.scalar.activation(out=table_out[:], in_=table_in[:], func=ACT.Gelu)
+
+        o_tiles = o_glob.rearrange("b n (h s) d -> b h s n d", s=P)
+        x_tiles = x_loc.flatten_outer_dims().rearrange("(i r) d -> r i d", r=P)
+        wo_blocks = Wo_g.rearrange("(c r) k -> r c k", r=P)
+        w1_blocks = W1.rearrange("(c r) k -> r c k", r=P)
+
+        def load_o_pair(first):
+            for i in (first, first + 1):
+                nc.sync.dma_start(
+                    out=o_rows[:, i, :].rearrange("s (n d) -> s n d", d=P),
+                    in_=o_tiles[i // 2, i % 2],
+                )
+
+        load_o_pair(0)
+        nc.sync.dma_start(out=wo_rows[:, :2, :], in_=wo_blocks[:, :2, :])
+        nc.sync.dma_start(out=wo_rows[:, 2:, :], in_=wo_blocks[:, 2:, :])
+        nc.sync.dma_start(out=bias_rows[0:1, :D], in_=bo_g.unsqueeze(0))
+        nc.sync.dma_start(out=bias_rows[0:1, D:], in_=b1.unsqueeze(0))
+        nc.sync.dma_start(out=x_rows[:, :4, :], in_=x_tiles[:, :4, :])
+        nc.sync.dma_start(out=ln_w_bf[:], in_=ln3_w.rearrange("(p t) -> p t", t=PACK))
+        nc.sync.dma_start(out=ln_b_bf[:], in_=ln3_b.rearrange("(p t) -> p t", t=PACK))
+        load_o_pair(2)
+        load_o_pair(4)
+        nc.sync.dma_start(out=x_rows[:, 4:, :], in_=x_tiles[:, 4:, :])
+        load_o_pair(6)
+        nc.sync.dma_start(out=w1_rows[:, :4, :], in_=w1_blocks[:, :4, :])
+        nc.sync.dma_start(out=w1_rows[:, 4:, :], in_=w1_blocks[:, 4:, :])
+
+        o_words = o_rows[:].bitcast(F32)
+        o_grouped_words = o_grouped[:].bitcast(F32)
+        wo_words = wo_rows[:].bitcast(F32)
+        wo_grouped_words = wo_grouped[:].bitcast(F32)
+        w1_words = w1_rows[:].bitcast(F32)
+        w1_grouped_words = w1_grouped[:].bitcast(F32)
+
+        def tokens(i):
+            return slice(i * P, (i + 1) * P)
+
+        def prepare_residual(i):
+            nc.vector.tensor_tensor(
+                out=x_glob[:, i, :], in0=x_rows[:, i, :], in1=bias_all[:, :D], op=ALU.add
             )
 
-            product = acc_one.tile([P, D], F32)
+        def project(i):
+            product = psum.tile([P, D], F32, tag="product", bufs=1)
             nc.tensor.matmul_mx(
                 out=product[:],
-                lhsT=o_codes[:, tokens].bitcast(FP8X4),
-                lhsT_scale=o_scales[:, tokens],
+                lhsT=o_codes[:, tokens(i)].bitcast(FP8X4),
+                lhsT_scale=o_scales[:, tokens(i)],
                 rhs=wo_codes[:].bitcast(FP8X4),
                 rhs_scale=wo_scales[:],
                 start=True,
                 stop=True,
             )
-            x_glob = work.tile([P, D], F32)
-            row_sum = stats.tile([P, 1], F32)
+            products[i] = product
+
+        def add_residual(i):
             nc.vector.scalar_tensor_tensor(
-                out=x_glob[:],
-                in0=product[:],
+                out=x_glob[:, i, :],
+                in0=products[i][:],
                 scalar=0.0,
-                in1=residual[:],
+                in1=x_glob[:, i, :],
                 op0=ALU.add,
                 op1=ALU.add,
-                accum_out=row_sum[:],
+                accum_out=row_sum[:, i : i + 1],
             )
-            nc.sync.dma_start(out=x_glob_out[tokens, :], in_=x_glob[:])
-
-            minus_mean = stats.tile([P, 1], F32)
+            nc.sync.dma_start(out=x_glob_out[tokens(i), :], in_=x_glob[:, i, :])
             nc.gpsimd.tensor_scalar(
-                out=minus_mean[:],
-                in0=row_sum[:],
+                out=minus_mean[:, i : i + 1],
+                in0=row_sum[:, i : i + 1],
                 scalar1=-1.0 / D,
                 scalar2=0.0,
                 op0=ALU.mult,
                 op1=ALU.add,
             )
-            squares = work.tile([P, D], BF16)
-            square_sum = stats.tile([P, 1], F32)
+
+        def deviations(i):
             nc.scalar.activation(
-                out=squares[:],
-                in_=x_glob[:],
+                out=squares[:, i, :],
+                in_=x_glob[:, i, :],
                 func=ACT.Square,
-                bias=minus_mean[:],
+                bias=minus_mean[:, i : i + 1],
                 scale=1.0,
-                accum_out=square_sum[:],
+                accum_out=square_sum[:, i : i + 1],
             )
-            var_eps = stats.tile([P, 1], F32)
             nc.gpsimd.tensor_scalar(
-                out=var_eps[:],
-                in0=square_sum[:],
+                out=var_eps[:, i : i + 1],
+                in0=square_sum[:, i : i + 1],
                 scalar1=1.0 / D,
                 scalar2=EPS,
                 op0=ALU.mult,
                 op1=ALU.add,
             )
-            inv_std = stats.tile([P, 1], F32)
             nc.gpsimd.tensor_tensor(
-                out=inv_std[:], in0=var_eps[:], in1=minus_half[:], op=ALU.pow
+                out=inv_std[:, i : i + 1],
+                in0=var_eps[:, i : i + 1],
+                in1=minus_half[:],
+                op=ALU.pow,
             )
 
-            centred = work.tile([P, PACK, P], F32)
+        def normalise(i):
             nc.vector.tensor_scalar(
-                out=centred[:],
-                in0=x_glob[:].rearrange("r (p t) -> r t p", t=PACK),
-                scalar1=minus_mean[:],
-                scalar2=inv_std[:],
+                out=centred[:, i, :, :],
+                in0=x_glob[:, i, :].rearrange("r (p t) -> r t p", t=PACK),
+                scalar1=minus_mean[:, i : i + 1],
+                scalar2=inv_std[:, i : i + 1],
                 op0=ALU.add,
                 op1=ALU.mult,
             )
-            centred_t = banks.tile([P, PACK, P], F32, tag="bank")
+            bank = psum.tile([P, PACK, P], F32, tag="bank", bufs=3)
             for t in range(PACK):
-                nc.tensor.transpose(centred_t[:, t, :], centred[:, t, :], identity[:])
-            h_planes = work.tile([P, PACK, P], BF16)
+                nc.tensor.transpose(bank[:, t, :], centred[:, i, t, :], identity[:])
+            flipped[i] = bank
+
+        def scale_shift(i):
             for t in range(PACK):
                 nc.scalar.activation(
-                    out=h_planes[:, t, :],
-                    in_=centred_t[:, t, :],
+                    out=h_planes[:, i, t, :],
+                    in_=flipped[i][:, t, :],
                     func=ACT.Identity,
                     scale=ln_w[:, t : t + 1],
                     bias=ln_b[:, t : t + 1],
                 )
-            h_grouped = work.tile([P, P, PACK], BF16, align_bytes=64)
-            nc.vector.tensor_copy(
-                out=h_grouped[:].rearrange("p (c i) t -> p c t i", i=4),
-                in_=h_planes[:].rearrange("p t (c i) -> p c t i", i=4),
-            )
-            h_codes = work.tile([P, P], U32, align_bytes=64)
-            h_scales = work.tile([P, P], U8, align_bytes=64)
-            quantise_rows(nc, h_grouped, h_codes, h_scales, 0, P)
 
-            g_tile = work.tile([P, F], F32)
+        def regroup(i):
+            nc.vector.tensor_copy(
+                out=h_grouped[:, tokens(i), :].rearrange("p (c i) t -> p c t i", i=4),
+                in_=h_planes[:, i, :, :].rearrange("p t (c i) -> p c t i", i=4),
+            )
+
+        def requantise(i):
+            quantise_rows(nc, h_grouped, h_codes, h_scales, i * P, P)
+
+        def up_project(i):
             for first in range(0, F, BANK):
-                features = slice(first, first + BANK)
-                up = acc_two.tile([P, BANK], F32)
+                up = psum.tile([P, BANK], F32, tag="up", bufs=4)
                 nc.tensor.matmul_mx(
                     out=up[:],
-                    lhsT=h_codes[:].bitcast(FP8X4),
-                    lhsT_scale=h_scales[:],
-                    rhs=w1_codes[:, features].bitcast(FP8X4),
-                    rhs_scale=w1_scales[:, features],
+                    lhsT=h_codes[:, tokens(i)].bitcast(FP8X4),
+                    lhsT_scale=h_scales[:, tokens(i)],
+                    rhs=w1_codes[:, first : first + BANK].bitcast(FP8X4),
+                    rhs_scale=w1_scales[:, first : first + BANK],
                     start=True,
                     stop=True,
                 )
-                biased = work.tile([P, BANK], F32, bufs=4)
+                ups[i, first] = up
+
+        def bias_gelu_store(i):
+            for first in range(0, F, BANK):
+                part = g[:, i, first : first + BANK]
                 nc.vector.tensor_tensor(
-                    out=biased[:], in0=up[:], in1=b1_all[:, features], op=ALU.add
+                    out=part,
+                    in0=ups[i, first][:],
+                    in1=bias_all[:, D + first : D + first + BANK],
+                    op=ALU.add,
                 )
-                nc.scalar.activation(out=g_tile[:, features], in_=biased[:], func=ACT.Gelu)
-            nc.sync.dma_start(out=g_out[tokens, :], in_=g_tile[:])
+                nc.scalar.activation(out=part, in_=part, func=ACT.Gelu)
+                nc.sync.dma_start(out=g_out[tokens(i), first : first + BANK], in_=part)
+
+        def run(stage, i):
+            if 0 <= i < TILES:
+                stage(i)
+
+        flip_two_blocks(nc, psum, identity, o_words, o_grouped_words, 0, nc.scalar.copy)
+        flip_two_blocks(nc, psum, identity, wo_words, wo_grouped_words, 0, nc.scalar.copy)
+        flip_two_blocks(nc, psum, identity, wo_words, wo_grouped_words, 2, nc.vector.tensor_copy)
+        quantise_rows(nc, o_grouped, o_codes, o_scales, 0, 2 * P)
+        quantise_rows(nc, wo_grouped, wo_codes, wo_scales, 0, D)
+        bo_bank = psum.tile([P, D], BF16, tag="bank", bufs=3)
+        nc.tensor.matmul(out=bo_bank[:], lhsT=ones[:], rhs=bias_rows[:, :D], start=True, stop=True)
+        nc.scalar.copy(out=bias_all[:, :D], in_=bo_bank[:])
+        b1_bank = psum.tile([P, F], BF16, tag="bank", bufs=3)
+        for first in range(0, F, BANK):
+            nc.tensor.matmul(
+                out=b1_bank[:, first : first + BANK],
+                lhsT=ones[:],
+                rhs=bias_rows[:, D + first : D + first + BANK],
+                start=True,
+                stop=True,
+            )
+        nc.scalar.copy(out=bias_all[:, D:], in_=b1_bank[:])
+        nc.gpsimd.tensor_copy(out=ln_w[:], in_=ln_w_bf[:])
+        nc.gpsimd.tensor_copy(out=ln_b[:], in_=ln_b_bf[:])
+        prepare_residual(0)
+
+        for step in range(TILES + LAST_LAG):
+            if step % 2 == 1 and step + 1 < TILES:
+                quantise_rows(nc, o_grouped, o_codes, o_scales, (step + 1) * P, 2 * P)
+            if step == 3 or step == 5:
+                quantise_rows(nc, w1_grouped, w1_codes, w1_scales, (step - 3) // 2 * BANK, BANK)
+            run(scale_shift, step - 4)
+            run(deviations, step - 2)
+            run(regroup, step - 5)
+            run(add_residual, step - 1)
+            run(project, step)
+            run(requantise, step - 5)
+            run(up_project, step - 5)
+            run(bias_gelu_store, step - LAST_LAG)
+            run(normalise, step - 3)
+            run(prepare_residual, step + 1)
+            if step % 2 == 0 and step + 2 < TILES:
+                flip_two_blocks(
+                    nc, psum, identity, o_words, o_grouped_words, step + 2, nc.scalar.copy
+                )
+            if 1 <= step <= 4:
+                flip_two_blocks(
+                    nc, psum, identity, w1_words, w1_grouped_words, 2 * (step - 1), nc.scalar.copy
+                )

@@ -28,9 +28,10 @@ FLOPS = 2 * TOKENS * K * D + 2 * TOKENS * K * F
 def flip_two_blocks(nc, psum, identity, rows, grouped, block, copy):
     bank = psum.tile([P, 2, 2, P], F32, tag="bank", bufs=3)
     for j in range(2):
-        pairs = rows[:, block + j, :].rearrange("r (p u) -> r p u", u=2)
         for u in range(2):
-            nc.tensor.transpose(bank[:, j, u, :], pairs[:, :, u], identity[:])
+            nc.tensor.transpose(
+                bank[:, j, u, :], rows[:, block + j, u * P : (u + 1) * P], identity[:]
+            )
     copy(
         out=grouped[:, block * P : (block + 2) * P, :].rearrange("p (j r) u -> p j r u", j=2),
         in_=bank[:].rearrange("p j u r -> p j r u"),
@@ -105,6 +106,16 @@ def tile_block_pb_kernel(
         nc.vector.memset(minus_half[:], -0.5)
         nc.vector.memset(table_in[:], 0.0)
         make_identity(nc, identity[:])
+        nc.scalar.dma_start(out=bias_rows[0:1, :D], in_=bo_g.unsqueeze(0))
+        nc.scalar.dma_start(out=bias_rows[0:1, D:], in_=b1.unsqueeze(0))
+        nc.scalar.dma_start(
+            out=ln_w_bf[:].rearrange("p (u e) -> p u e", e=2),
+            in_=ln3_w.rearrange("(u p e) -> p u e", u=2, e=2),
+        )
+        nc.scalar.dma_start(
+            out=ln_b_bf[:].rearrange("p (u e) -> p u e", e=2),
+            in_=ln3_b.rearrange("(u p e) -> p u e", u=2, e=2),
+        )
         nc.scalar.activation(out=table_out[:], in_=table_in[:], func=ACT.Gelu)
 
         o_tiles = o_glob.rearrange("b n (h s) d -> b h s n d", s=P)
@@ -122,11 +133,7 @@ def tile_block_pb_kernel(
         load_o_pair(0)
         nc.sync.dma_start(out=wo_rows[:, :2, :], in_=wo_blocks[:, :2, :])
         nc.sync.dma_start(out=wo_rows[:, 2:, :], in_=wo_blocks[:, 2:, :])
-        nc.sync.dma_start(out=bias_rows[0:1, :D], in_=bo_g.unsqueeze(0))
-        nc.sync.dma_start(out=bias_rows[0:1, D:], in_=b1.unsqueeze(0))
         nc.sync.dma_start(out=x_rows[:, :4, :], in_=x_tiles[:, :4, :])
-        nc.sync.dma_start(out=ln_w_bf[:], in_=ln3_w.rearrange("(p t) -> p t", t=PACK))
-        nc.sync.dma_start(out=ln_b_bf[:], in_=ln3_b.rearrange("(p t) -> p t", t=PACK))
         load_o_pair(2)
         load_o_pair(4)
         nc.sync.dma_start(out=x_rows[:, 4:, :], in_=x_tiles[:, 4:, :])
@@ -208,8 +215,8 @@ def tile_block_pb_kernel(
 
         def normalise(i):
             nc.vector.tensor_scalar(
-                out=centred[:, i, :, :],
-                in0=x_glob[:, i, :].rearrange("r (p t) -> r t p", t=PACK),
+                out=centred[:, i, :, :].rearrange("r (u e) p -> r u e p", e=2),
+                in0=x_glob[:, i, :].rearrange("r (u p e) -> r u e p", u=2, e=2),
                 scalar1=minus_mean[:, i : i + 1],
                 scalar2=inv_std[:, i : i + 1],
                 op0=ALU.add,
@@ -269,11 +276,6 @@ def tile_block_pb_kernel(
             if 0 <= i < TILES:
                 stage(i)
 
-        flip_two_blocks(nc, psum, identity, o_words, o_grouped_words, 0, nc.scalar.copy)
-        flip_two_blocks(nc, psum, identity, wo_words, wo_grouped_words, 0, nc.scalar.copy)
-        flip_two_blocks(nc, psum, identity, wo_words, wo_grouped_words, 2, nc.vector.tensor_copy)
-        quantise_rows(nc, o_grouped, o_codes, o_scales, 0, 2 * P)
-        quantise_rows(nc, wo_grouped, wo_codes, wo_scales, 0, D)
         bo_bank = psum.tile([P, D], BF16, tag="bank", bufs=3)
         nc.tensor.matmul(out=bo_bank[:], lhsT=ones[:], rhs=bias_rows[:, :D], start=True, stop=True)
         nc.scalar.copy(out=bias_all[:, :D], in_=bo_bank[:])
@@ -287,6 +289,11 @@ def tile_block_pb_kernel(
                 stop=True,
             )
         nc.scalar.copy(out=bias_all[:, D:], in_=b1_bank[:])
+        flip_two_blocks(nc, psum, identity, o_words, o_grouped_words, 0, nc.scalar.copy)
+        flip_two_blocks(nc, psum, identity, wo_words, wo_grouped_words, 0, nc.scalar.copy)
+        flip_two_blocks(nc, psum, identity, wo_words, wo_grouped_words, 2, nc.vector.tensor_copy)
+        quantise_rows(nc, o_grouped, o_codes, o_scales, 0, 2 * P)
+        quantise_rows(nc, wo_grouped, wo_codes, wo_scales, 0, D)
         nc.gpsimd.tensor_copy(out=ln_w[:], in_=ln_w_bf[:])
         nc.gpsimd.tensor_copy(out=ln_b[:], in_=ln_b_bf[:])
         prepare_residual(0)

@@ -106,16 +106,6 @@ def tile_block_pb_kernel(
         nc.vector.memset(minus_half[:], -0.5)
         nc.vector.memset(table_in[:], 0.0)
         make_identity(nc, identity[:])
-        nc.scalar.dma_start(out=bias_rows[0:1, :D], in_=bo_g.unsqueeze(0))
-        nc.scalar.dma_start(out=bias_rows[0:1, D:], in_=b1.unsqueeze(0))
-        nc.scalar.dma_start(
-            out=ln_w_bf[:].rearrange("p (u e) -> p u e", e=2),
-            in_=ln3_w.rearrange("(u p e) -> p u e", u=2, e=2),
-        )
-        nc.scalar.dma_start(
-            out=ln_b_bf[:].rearrange("p (u e) -> p u e", e=2),
-            in_=ln3_b.rearrange("(u p e) -> p u e", u=2, e=2),
-        )
         nc.scalar.activation(out=table_out[:], in_=table_in[:], func=ACT.Gelu)
 
         o_tiles = o_glob.rearrange("b n (h s) d -> b h s n d", s=P)
@@ -130,10 +120,20 @@ def tile_block_pb_kernel(
                     in_=o_tiles[i // 2, i % 2],
                 )
 
-        load_o_pair(0)
         nc.sync.dma_start(out=wo_rows[:, :2, :], in_=wo_blocks[:, :2, :])
         nc.sync.dma_start(out=wo_rows[:, 2:, :], in_=wo_blocks[:, 2:, :])
+        load_o_pair(0)
+        nc.sync.dma_start(out=bias_rows[0:1, :D], in_=bo_g.unsqueeze(0))
+        nc.sync.dma_start(out=bias_rows[0:1, D:], in_=b1.unsqueeze(0))
         nc.sync.dma_start(out=x_rows[:, :4, :], in_=x_tiles[:, :4, :])
+        nc.sync.dma_start(
+            out=ln_w_bf[:].rearrange("p (u e) -> p u e", e=2),
+            in_=ln3_w.rearrange("(u p e) -> p u e", u=2, e=2),
+        )
+        nc.sync.dma_start(
+            out=ln_b_bf[:].rearrange("p (u e) -> p u e", e=2),
+            in_=ln3_b.rearrange("(u p e) -> p u e", u=2, e=2),
+        )
         load_o_pair(2)
         load_o_pair(4)
         nc.sync.dma_start(out=x_rows[:, 4:, :], in_=x_tiles[:, 4:, :])
@@ -194,14 +194,14 @@ def tile_block_pb_kernel(
                 out=squares[:, i, :],
                 in_=x_glob[:, i, :],
                 func=ACT.Square,
-                bias=minus_mean[:, i : i + 1],
-                scale=1.0,
+                bias=row_sum[:, i : i + 1],
+                scale=-1.0 * D,
                 accum_out=square_sum[:, i : i + 1],
             )
             nc.gpsimd.tensor_scalar(
                 out=var_eps[:, i : i + 1],
                 in0=square_sum[:, i : i + 1],
-                scalar1=1.0 / D,
+                scalar1=1.0 / (D * D * D),
                 scalar2=EPS,
                 op0=ALU.mult,
                 op1=ALU.add,
@@ -276,6 +276,11 @@ def tile_block_pb_kernel(
             if 0 <= i < TILES:
                 stage(i)
 
+        flip_two_blocks(nc, psum, identity, wo_words, wo_grouped_words, 0, nc.scalar.copy)
+        flip_two_blocks(nc, psum, identity, wo_words, wo_grouped_words, 2, nc.vector.tensor_copy)
+        flip_two_blocks(nc, psum, identity, o_words, o_grouped_words, 0, nc.scalar.copy)
+        quantise_rows(nc, wo_grouped, wo_codes, wo_scales, 0, D)
+        quantise_rows(nc, o_grouped, o_codes, o_scales, 0, 2 * P)
         bo_bank = psum.tile([P, D], BF16, tag="bank", bufs=3)
         nc.tensor.matmul(out=bo_bank[:], lhsT=ones[:], rhs=bias_rows[:, :D], start=True, stop=True)
         nc.scalar.copy(out=bias_all[:, :D], in_=bo_bank[:])
@@ -289,11 +294,6 @@ def tile_block_pb_kernel(
                 stop=True,
             )
         nc.scalar.copy(out=bias_all[:, D:], in_=b1_bank[:])
-        flip_two_blocks(nc, psum, identity, o_words, o_grouped_words, 0, nc.scalar.copy)
-        flip_two_blocks(nc, psum, identity, wo_words, wo_grouped_words, 0, nc.scalar.copy)
-        flip_two_blocks(nc, psum, identity, wo_words, wo_grouped_words, 2, nc.vector.tensor_copy)
-        quantise_rows(nc, o_grouped, o_codes, o_scales, 0, 2 * P)
-        quantise_rows(nc, wo_grouped, wo_codes, wo_scales, 0, D)
         nc.gpsimd.tensor_copy(out=ln_w[:], in_=ln_w_bf[:])
         nc.gpsimd.tensor_copy(out=ln_b[:], in_=ln_b_bf[:])
         prepare_residual(0)

@@ -26,7 +26,7 @@ FLOPS = 2 * TOKENS * K * D + 2 * TOKENS * K * F
 
 
 def flip_two_blocks(nc, psum, identity, rows, grouped, block, copy):
-    bank = psum.tile([P, 2, 2, P], F32, tag="bank", bufs=3)
+    bank = psum.tile([P, 2, 2, P], F32, tag="bank", bufs=4)
     for j in range(2):
         for u in range(2):
             nc.tensor.transpose(
@@ -56,6 +56,7 @@ def tile_block_pb_kernel(
     with ExitStack() as stack:
         keep = stack.enter_context(tc.tile_pool(name="keep", bufs=1))
         psum = stack.enter_context(tc.psum_pool(name="psum", bufs=2))
+        stack.enter_context(tc.manual_schedule())
 
         wo_rows = keep.tile([P, D // P, K], BF16)
         o_rows = keep.tile([P, TILES, K], BF16)
@@ -120,12 +121,17 @@ def tile_block_pb_kernel(
                     in_=o_tiles[i // 2, i % 2],
                 )
 
+        def load_x_pair(first):
+            nc.sync.dma_start(
+                out=x_rows[:, first : first + 2, :], in_=x_tiles[:, first : first + 2, :]
+            )
+
         nc.sync.dma_start(out=wo_rows[:, :2, :], in_=wo_blocks[:, :2, :])
         nc.sync.dma_start(out=wo_rows[:, 2:, :], in_=wo_blocks[:, 2:, :])
         load_o_pair(0)
         nc.sync.dma_start(out=bias_rows[0:1, :D], in_=bo_g.unsqueeze(0))
         nc.sync.dma_start(out=bias_rows[0:1, D:], in_=b1.unsqueeze(0))
-        nc.sync.dma_start(out=x_rows[:, :4, :], in_=x_tiles[:, :4, :])
+        load_x_pair(0)
         nc.sync.dma_start(
             out=ln_w_bf[:].rearrange("p (u e) -> p u e", e=2),
             in_=ln3_w.rearrange("(u p e) -> p u e", u=2, e=2),
@@ -134,10 +140,9 @@ def tile_block_pb_kernel(
             out=ln_b_bf[:].rearrange("p (u e) -> p u e", e=2),
             in_=ln3_b.rearrange("(u p e) -> p u e", u=2, e=2),
         )
-        load_o_pair(2)
-        load_o_pair(4)
-        nc.sync.dma_start(out=x_rows[:, 4:, :], in_=x_tiles[:, 4:, :])
-        load_o_pair(6)
+        for pair in (2, 4, 6):
+            load_o_pair(pair)
+            load_x_pair(pair)
         nc.sync.dma_start(out=w1_rows[:, :4, :], in_=w1_blocks[:, :4, :])
         nc.sync.dma_start(out=w1_rows[:, 4:, :], in_=w1_blocks[:, 4:, :])
 
@@ -157,7 +162,7 @@ def tile_block_pb_kernel(
             )
 
         def project(i):
-            product = psum.tile([P, D], F32, tag="product", bufs=1)
+            product = psum.tile([P, D], F32, tag="product", bufs=2)
             nc.tensor.matmul_mx(
                 out=product[:],
                 lhsT=o_codes[:, tokens(i)].bitcast(FP8X4),
@@ -222,7 +227,7 @@ def tile_block_pb_kernel(
                 op0=ALU.add,
                 op1=ALU.mult,
             )
-            bank = psum.tile([P, PACK, P], F32, tag="bank", bufs=3)
+            bank = psum.tile([P, PACK, P], F32, tag="bank", bufs=4)
             for t in range(PACK):
                 nc.tensor.transpose(bank[:, t, :], centred[:, i, t, :], identity[:])
             flipped[i] = bank
@@ -248,7 +253,7 @@ def tile_block_pb_kernel(
 
         def up_project(i):
             for first in range(0, F, BANK):
-                up = psum.tile([P, BANK], F32, tag="up", bufs=4)
+                up = psum.tile([P, BANK], F32, tag="up", bufs=2)
                 nc.tensor.matmul_mx(
                     out=up[:],
                     lhsT=h_codes[:, tokens(i)].bitcast(FP8X4),
@@ -280,11 +285,10 @@ def tile_block_pb_kernel(
         flip_two_blocks(nc, psum, identity, wo_words, wo_grouped_words, 2, nc.vector.tensor_copy)
         flip_two_blocks(nc, psum, identity, o_words, o_grouped_words, 0, nc.scalar.copy)
         quantise_rows(nc, wo_grouped, wo_codes, wo_scales, 0, D)
-        quantise_rows(nc, o_grouped, o_codes, o_scales, 0, 2 * P)
-        bo_bank = psum.tile([P, D], BF16, tag="bank", bufs=3)
+        bo_bank = psum.tile([P, D], BF16, tag="bank", bufs=4)
         nc.tensor.matmul(out=bo_bank[:], lhsT=ones[:], rhs=bias_rows[:, :D], start=True, stop=True)
         nc.scalar.copy(out=bias_all[:, :D], in_=bo_bank[:])
-        b1_bank = psum.tile([P, F], BF16, tag="bank", bufs=3)
+        b1_bank = psum.tile([P, F], BF16, tag="bank", bufs=4)
         for first in range(0, F, BANK):
             nc.tensor.matmul(
                 out=b1_bank[:, first : first + BANK],
@@ -296,28 +300,32 @@ def tile_block_pb_kernel(
         nc.scalar.copy(out=bias_all[:, D:], in_=b1_bank[:])
         nc.gpsimd.tensor_copy(out=ln_w[:], in_=ln_w_bf[:])
         nc.gpsimd.tensor_copy(out=ln_b[:], in_=ln_b_bf[:])
+        flip_two_blocks(nc, psum, identity, o_words, o_grouped_words, 2, nc.scalar.copy)
+        quantise_rows(nc, o_grouped, o_codes, o_scales, 0, 2 * P)
         prepare_residual(0)
+        prepare_residual(1)
+        project(0)
 
         for step in range(TILES + LAST_LAG):
-            if step % 2 == 1 and step + 1 < TILES:
-                quantise_rows(nc, o_grouped, o_codes, o_scales, (step + 1) * P, 2 * P)
-            if step == 3 or step == 5:
-                quantise_rows(nc, w1_grouped, w1_codes, w1_scales, (step - 3) // 2 * BANK, BANK)
-            run(scale_shift, step - 4)
-            run(deviations, step - 2)
-            run(regroup, step - 5)
-            run(add_residual, step - 1)
-            run(project, step)
-            run(requantise, step - 5)
-            run(up_project, step - 5)
-            run(bias_gelu_store, step - LAST_LAG)
-            run(normalise, step - 3)
-            run(prepare_residual, step + 1)
+            run(project, step + 1)
+            run(add_residual, step)
             if step % 2 == 0 and step + 2 < TILES:
-                flip_two_blocks(
-                    nc, psum, identity, o_words, o_grouped_words, step + 2, nc.scalar.copy
-                )
+                quantise_rows(nc, o_grouped, o_codes, o_scales, (step + 2) * P, 2 * P)
+            run(scale_shift, step - 3)
+            run(deviations, step)
+            run(normalise, step - 2)
+            run(regroup, step - 4)
+            run(prepare_residual, step + 2)
+            run(requantise, step - 4)
+            if step == 4 or step == 5:
+                quantise_rows(nc, w1_grouped, w1_codes, w1_scales, (step - 4) * BANK, BANK)
+            run(bias_gelu_store, step - LAST_LAG)
+            run(up_project, step - 5)
             if 1 <= step <= 4:
                 flip_two_blocks(
                     nc, psum, identity, w1_words, w1_grouped_words, 2 * (step - 1), nc.scalar.copy
+                )
+            if step % 2 == 0 and step + 4 < TILES:
+                flip_two_blocks(
+                    nc, psum, identity, o_words, o_grouped_words, step + 4, nc.scalar.copy
                 )

@@ -265,21 +265,20 @@ def tile_block_pb_kernel(
                 )
                 ups[i, first] = up
 
-        def bias_gelu_store(i):
-            for first in range(0, F, BANK):
-                part = g[:, i, first : first + BANK]
-                nc.vector.tensor_tensor(
-                    out=part,
-                    in0=ups[i, first][:],
-                    in1=bias_all[:, D + first : D + first + BANK],
-                    op=ALU.add,
-                )
-                nc.scalar.activation(out=part, in_=part, func=ACT.Gelu)
-                nc.sync.dma_start(out=g_out[tokens(i), first : first + BANK], in_=part)
+        def bias_gelu_store(i, first):
+            part = g[:, i, first : first + BANK]
+            nc.vector.tensor_tensor(
+                out=part,
+                in0=ups[i, first][:],
+                in1=bias_all[:, D + first : D + first + BANK],
+                op=ALU.add,
+            )
+            nc.scalar.activation(out=part, in_=part, func=ACT.Gelu)
+            nc.sync.dma_start(out=g_out[tokens(i), first : first + BANK], in_=part)
 
-        def run(stage, i):
+        def run(stage, i, *rest):
             if 0 <= i < TILES:
-                stage(i)
+                stage(i, *rest)
 
         flip_two_blocks(nc, psum, identity, wo_words, wo_grouped_words, 0, nc.scalar.copy)
         flip_two_blocks(nc, psum, identity, wo_words, wo_grouped_words, 2, nc.vector.tensor_copy)
@@ -315,11 +314,12 @@ def tile_block_pb_kernel(
             run(deviations, step)
             run(normalise, step - 2)
             run(regroup, step - 4)
+            run(bias_gelu_store, step - LAST_LAG, 0)
             run(prepare_residual, step + 2)
             run(requantise, step - 4)
             if step == 4 or step == 5:
                 quantise_rows(nc, w1_grouped, w1_codes, w1_scales, (step - 4) * BANK, BANK)
-            run(bias_gelu_store, step - LAST_LAG)
+            run(bias_gelu_store, step - LAST_LAG, BANK)
             run(up_project, step - 5)
             if 1 <= step <= 4:
                 flip_two_blocks(

@@ -25,15 +25,17 @@ LAST_LAG = 6
 FLOPS = 2 * TOKENS * K * D + 2 * TOKENS * K * F
 
 
-def flip_two_blocks(nc, psum, identity, rows, grouped, block, copy):
-    bank = psum.tile([P, 2, 2, P], F32, tag="bank", bufs=4)
-    for j in range(2):
+def flip_blocks(nc, psum, identity, rows, grouped, block, count, copy):
+    bank = psum.tile([P, count, 2, P], F32, tag="bank", bufs=4)
+    for j in range(count):
         for u in range(2):
             nc.tensor.transpose(
                 bank[:, j, u, :], rows[:, block + j, u * P : (u + 1) * P], identity[:]
             )
     copy(
-        out=grouped[:, block * P : (block + 2) * P, :].rearrange("p (j r) u -> p j r u", j=2),
+        out=grouped[:, block * P : (block + count) * P, :].rearrange(
+            "p (j r) u -> p j r u", j=count
+        ),
         in_=bank[:].rearrange("p j u r -> p j r u"),
     )
 
@@ -126,8 +128,8 @@ def tile_block_pb_kernel(
                 out=x_rows[:, first : first + 2, :], in_=x_tiles[:, first : first + 2, :]
             )
 
-        nc.sync.dma_start(out=wo_rows[:, :2, :], in_=wo_blocks[:, :2, :])
-        nc.sync.dma_start(out=wo_rows[:, 2:, :], in_=wo_blocks[:, 2:, :])
+        for block in range(D // P):
+            nc.sync.dma_start(out=wo_rows[:, block, :], in_=wo_blocks[:, block, :])
         load_o_pair(0)
         nc.sync.dma_start(out=bias_rows[0:1, :D], in_=bo_g.unsqueeze(0))
         nc.sync.dma_start(out=bias_rows[0:1, D:], in_=b1.unsqueeze(0))
@@ -266,40 +268,45 @@ def tile_block_pb_kernel(
                 ups[i, first] = up
 
         def bias_gelu_store(i, first):
-            part = g[:, i, first : first + BANK]
-            nc.vector.tensor_tensor(
-                out=part,
-                in0=ups[i, first][:],
-                in1=bias_all[:, D + first : D + first + BANK],
-                op=ALU.add,
-            )
-            nc.scalar.activation(out=part, in_=part, func=ACT.Gelu)
-            nc.sync.dma_start(out=g_out[tokens(i), first : first + BANK], in_=part)
+            width = BANK // 2 if (i, first) == (TILES - 1, F - BANK) else BANK
+            for start in range(first, first + BANK, width):
+                part = g[:, i, start : start + width]
+                nc.vector.tensor_tensor(
+                    out=part,
+                    in0=ups[i, first][:, start - first : start - first + width],
+                    in1=bias_all[:, D + start : D + start + width],
+                    op=ALU.add,
+                )
+                nc.scalar.activation(out=part, in_=part, func=ACT.Gelu)
+                nc.sync.dma_start(out=g_out[tokens(i), start : start + width], in_=part)
+
+        def spread_b1():
+            b1_bank = psum.tile([P, F], BF16, tag="bank", bufs=4)
+            for first in range(0, F, BANK):
+                nc.tensor.matmul(
+                    out=b1_bank[:, first : first + BANK],
+                    lhsT=ones[:],
+                    rhs=bias_rows[:, D + first : D + first + BANK],
+                    start=True,
+                    stop=True,
+                )
+            nc.scalar.copy(out=bias_all[:, D:], in_=b1_bank[:])
 
         def run(stage, i, *rest):
             if 0 <= i < TILES:
                 stage(i, *rest)
 
-        flip_two_blocks(nc, psum, identity, wo_words, wo_grouped_words, 0, nc.scalar.copy)
-        flip_two_blocks(nc, psum, identity, wo_words, wo_grouped_words, 2, nc.vector.tensor_copy)
-        flip_two_blocks(nc, psum, identity, o_words, o_grouped_words, 0, nc.scalar.copy)
+        for block in range(D // P):
+            copy = nc.vector.tensor_copy if block % 2 else nc.scalar.copy
+            flip_blocks(nc, psum, identity, wo_words, wo_grouped_words, block, 1, copy)
+        flip_blocks(nc, psum, identity, o_words, o_grouped_words, 0, 2, nc.scalar.copy)
         quantise_rows(nc, wo_grouped, wo_codes, wo_scales, 0, D)
         bo_bank = psum.tile([P, D], BF16, tag="bank", bufs=4)
         nc.tensor.matmul(out=bo_bank[:], lhsT=ones[:], rhs=bias_rows[:, :D], start=True, stop=True)
         nc.scalar.copy(out=bias_all[:, :D], in_=bo_bank[:])
-        b1_bank = psum.tile([P, F], BF16, tag="bank", bufs=4)
-        for first in range(0, F, BANK):
-            nc.tensor.matmul(
-                out=b1_bank[:, first : first + BANK],
-                lhsT=ones[:],
-                rhs=bias_rows[:, D + first : D + first + BANK],
-                start=True,
-                stop=True,
-            )
-        nc.scalar.copy(out=bias_all[:, D:], in_=b1_bank[:])
         nc.gpsimd.tensor_copy(out=ln_w[:], in_=ln_w_bf[:])
         nc.gpsimd.tensor_copy(out=ln_b[:], in_=ln_b_bf[:])
-        flip_two_blocks(nc, psum, identity, o_words, o_grouped_words, 2, nc.scalar.copy)
+        flip_blocks(nc, psum, identity, o_words, o_grouped_words, 2, 2, nc.scalar.copy)
         quantise_rows(nc, o_grouped, o_codes, o_scales, 0, 2 * P)
         prepare_residual(0)
         prepare_residual(1)
@@ -321,11 +328,13 @@ def tile_block_pb_kernel(
                 quantise_rows(nc, w1_grouped, w1_codes, w1_scales, (step - 4) * BANK, BANK)
             run(bias_gelu_store, step - LAST_LAG, BANK)
             run(up_project, step - 5)
-            if 1 <= step <= 4:
-                flip_two_blocks(
-                    nc, psum, identity, w1_words, w1_grouped_words, 2 * (step - 1), nc.scalar.copy
+            if step == 1:
+                spread_b1()
+            for block in {2: (0,), 3: (2,), 4: (4, 6)}.get(step, ()):
+                flip_blocks(
+                    nc, psum, identity, w1_words, w1_grouped_words, block, 2, nc.scalar.copy
                 )
             if step % 2 == 0 and step + 4 < TILES:
-                flip_two_blocks(
-                    nc, psum, identity, o_words, o_grouped_words, step + 4, nc.scalar.copy
+                flip_blocks(
+                    nc, psum, identity, o_words, o_grouped_words, step + 4, 2, nc.scalar.copy
                 )

@@ -64,10 +64,9 @@ def tile_block_pb_kernel(
         o_rows = keep.tile([P, TILES, K], BF16)
         x_rows = keep.tile([P, TILES, D], BF16)
         w1_rows = keep.tile([P, F // P, K], BF16)
-        ln_w_bf = keep.tile([P, PACK], BF16)
-        ln_b_bf = keep.tile([P, PACK], BF16)
-        ln_w = keep.tile([P, PACK], F32)
-        ln_b = keep.tile([P, PACK], F32)
+        ln_rows = keep.tile([P, P], F32)
+        ln_words = keep.tile([P, PACK], F32)
+        ln_affine = keep.tile([P, 2 * PACK], F32)
         bias_rows = keep.tile([P, D + F], BF16)
         bias_all = keep.tile([P, D + F], BF16)
         ones = keep.tile([P, P], BF16)
@@ -104,6 +103,7 @@ def tile_block_pb_kernel(
         flipped = {}
         ups = {}
 
+        nc.vector.memset(ln_rows[:], 0.0)
         nc.vector.memset(bias_rows[:], 0.0)
         nc.vector.memset(ones[:], 1.0)
         nc.vector.memset(minus_half[:], -0.5)
@@ -135,12 +135,10 @@ def tile_block_pb_kernel(
         nc.sync.dma_start(out=bias_rows[0:1, D:], in_=b1.unsqueeze(0))
         load_x_pair(0)
         nc.sync.dma_start(
-            out=ln_w_bf[:].rearrange("p (u e) -> p u e", e=2),
-            in_=ln3_w.rearrange("(u p e) -> p u e", u=2, e=2),
+            out=ln_rows[0:2, :].bitcast(BF16), in_=ln3_w.rearrange("(u w) -> u w", u=2)
         )
         nc.sync.dma_start(
-            out=ln_b_bf[:].rearrange("p (u e) -> p u e", e=2),
-            in_=ln3_b.rearrange("(u p e) -> p u e", u=2, e=2),
+            out=ln_rows[2:4, :].bitcast(BF16), in_=ln3_b.rearrange("(u w) -> u w", u=2)
         )
         for pair in (2, 4, 6):
             load_o_pair(pair)
@@ -240,8 +238,8 @@ def tile_block_pb_kernel(
                     out=h_planes[:, i, t, :],
                     in_=flipped[i][:, t, :],
                     func=ACT.Identity,
-                    scale=ln_w[:, t : t + 1],
-                    bias=ln_b[:, t : t + 1],
+                    scale=ln_affine[:, t : t + 1],
+                    bias=ln_affine[:, PACK + t : PACK + t + 1],
                 )
 
         def regroup(i):
@@ -292,6 +290,12 @@ def tile_block_pb_kernel(
                 )
             nc.scalar.copy(out=bias_all[:, D:], in_=b1_bank[:])
 
+        def turn_ln_vectors():
+            bank = psum.tile([P, P], F32, tag="bank", bufs=4)
+            nc.tensor.transpose(bank[:], ln_rows[:], identity[:])
+            nc.scalar.copy(out=ln_words[:], in_=bank[:, :PACK])
+            nc.gpsimd.tensor_copy(out=ln_affine[:], in_=ln_words[:].bitcast(BF16))
+
         def run(stage, i, *rest):
             if 0 <= i < TILES:
                 stage(i, *rest)
@@ -304,8 +308,6 @@ def tile_block_pb_kernel(
         bo_bank = psum.tile([P, D], BF16, tag="bank", bufs=4)
         nc.tensor.matmul(out=bo_bank[:], lhsT=ones[:], rhs=bias_rows[:, :D], start=True, stop=True)
         nc.scalar.copy(out=bias_all[:, :D], in_=bo_bank[:])
-        nc.gpsimd.tensor_copy(out=ln_w[:], in_=ln_w_bf[:])
-        nc.gpsimd.tensor_copy(out=ln_b[:], in_=ln_b_bf[:])
         flip_blocks(nc, psum, identity, o_words, o_grouped_words, 2, 2, nc.scalar.copy)
         quantise_rows(nc, o_grouped, o_codes, o_scales, 0, 2 * P)
         prepare_residual(0)
@@ -330,6 +332,7 @@ def tile_block_pb_kernel(
             run(up_project, step - 5)
             if step == 1:
                 spread_b1()
+                turn_ln_vectors()
             for block in {2: (0,), 3: (2,), 4: (4, 6)}.get(step, ()):
                 flip_blocks(
                     nc, psum, identity, w1_words, w1_grouped_words, block, 2, nc.scalar.copy

@@ -67,7 +67,8 @@ def tile_block_pb_kernel(
         ln_rows = keep.tile([P, P], F32)
         ln_words = keep.tile([P, PACK], F32)
         ln_affine = keep.tile([P, 2 * PACK], F32)
-        bias_rows = keep.tile([P, D + F], BF16)
+        bo_rows = keep.tile([P, D], BF16)
+        b1_rows = keep.tile([P, F], BF16)
         bias_all = keep.tile([P, D + F], BF16)
         ones = keep.tile([P, P], BF16)
         identity = keep.tile([P, P], F32)
@@ -103,8 +104,9 @@ def tile_block_pb_kernel(
         flipped = {}
         ups = {}
 
+        nc.vector.memset(bo_rows[:], 0.0)
         nc.vector.memset(ln_rows[:], 0.0)
-        nc.vector.memset(bias_rows[:], 0.0)
+        nc.vector.memset(b1_rows[:], 0.0)
         nc.vector.memset(ones[:], 1.0)
         nc.vector.memset(minus_half[:], -0.5)
         nc.vector.memset(table_in[:], 0.0)
@@ -128,19 +130,17 @@ def tile_block_pb_kernel(
                 out=x_rows[:, first : first + 2, :], in_=x_tiles[:, first : first + 2, :]
             )
 
-        for block in range(D // P):
-            nc.sync.dma_start(out=wo_rows[:, block, :], in_=wo_blocks[:, block, :])
-        load_o_pair(0)
-        nc.sync.dma_start(out=bias_rows[0:1, :D], in_=bo_g.unsqueeze(0))
-        nc.sync.dma_start(out=bias_rows[0:1, D:], in_=b1.unsqueeze(0))
-        load_x_pair(0)
-        nc.sync.dma_start(
+        nc.gpsimd.dma_start(out=b1_rows[0:1, :], in_=b1.unsqueeze(0))
+        nc.gpsimd.dma_start(
             out=ln_rows[0:2, :].bitcast(BF16), in_=ln3_w.rearrange("(u w) -> u w", u=2)
         )
-        nc.sync.dma_start(
+        nc.gpsimd.dma_start(
             out=ln_rows[2:4, :].bitcast(BF16), in_=ln3_b.rearrange("(u w) -> u w", u=2)
         )
-        for pair in (2, 4, 6):
+        nc.sync.dma_start(out=wo_rows[:, :2, :], in_=wo_blocks[:, :2, :])
+        nc.sync.dma_start(out=wo_rows[:, 2:, :], in_=wo_blocks[:, 2:, :])
+        nc.sync.dma_start(out=bo_rows[0:1, :], in_=bo_g.unsqueeze(0))
+        for pair in range(0, TILES, 2):
             load_o_pair(pair)
             load_x_pair(pair)
         nc.sync.dma_start(out=w1_rows[:, :4, :], in_=w1_blocks[:, :4, :])
@@ -284,7 +284,7 @@ def tile_block_pb_kernel(
                 nc.tensor.matmul(
                     out=b1_bank[:, first : first + BANK],
                     lhsT=ones[:],
-                    rhs=bias_rows[:, D + first : D + first + BANK],
+                    rhs=b1_rows[:, first : first + BANK],
                     start=True,
                     stop=True,
                 )
@@ -306,7 +306,7 @@ def tile_block_pb_kernel(
         flip_blocks(nc, psum, identity, o_words, o_grouped_words, 0, 2, nc.scalar.copy)
         quantise_rows(nc, wo_grouped, wo_codes, wo_scales, 0, D)
         bo_bank = psum.tile([P, D], BF16, tag="bank", bufs=4)
-        nc.tensor.matmul(out=bo_bank[:], lhsT=ones[:], rhs=bias_rows[:, :D], start=True, stop=True)
+        nc.tensor.matmul(out=bo_bank[:], lhsT=ones[:], rhs=bo_rows[:], start=True, stop=True)
         nc.scalar.copy(out=bias_all[:, :D], in_=bo_bank[:])
         flip_blocks(nc, psum, identity, o_words, o_grouped_words, 2, 2, nc.scalar.copy)
         quantise_rows(nc, o_grouped, o_codes, o_scales, 0, 2 * P)

@@ -130,13 +130,13 @@ def tile_block_pb_kernel(
                 out=x_rows[:, first : first + 2, :], in_=x_tiles[:, first : first + 2, :]
             )
 
-        nc.gpsimd.dma_start(out=b1_rows[0:1, :], in_=b1.unsqueeze(0))
         nc.gpsimd.dma_start(
             out=ln_rows[0:2, :].bitcast(BF16), in_=ln3_w.rearrange("(u w) -> u w", u=2)
         )
         nc.gpsimd.dma_start(
             out=ln_rows[2:4, :].bitcast(BF16), in_=ln3_b.rearrange("(u w) -> u w", u=2)
         )
+        nc.gpsimd.dma_start(out=b1_rows[0:1, :], in_=b1.unsqueeze(0))
         nc.sync.dma_start(out=wo_rows[:, :2, :], in_=wo_blocks[:, :2, :])
         nc.sync.dma_start(out=wo_rows[:, 2:, :], in_=wo_blocks[:, 2:, :])
         nc.sync.dma_start(out=bo_rows[0:1, :], in_=bo_g.unsqueeze(0))
@@ -162,7 +162,7 @@ def tile_block_pb_kernel(
             )
 
         def project(i):
-            product = psum.tile([P, D], F32, tag="product", bufs=2)
+            product = psum.tile([P, D], F32, tag="mx", bufs=4)
             nc.tensor.matmul_mx(
                 out=product[:],
                 lhsT=o_codes[:, tokens(i)].bitcast(FP8X4),
@@ -253,7 +253,7 @@ def tile_block_pb_kernel(
 
         def up_project(i):
             for first in range(0, F, BANK):
-                up = psum.tile([P, BANK], F32, tag="up", bufs=2)
+                up = psum.tile([P, BANK], F32, tag="mx", bufs=4)
                 nc.tensor.matmul_mx(
                     out=up[:],
                     lhsT=h_codes[:, tokens(i)].bitcast(FP8X4),
@@ -326,14 +326,14 @@ def tile_block_pb_kernel(
             run(bias_gelu_store, step - LAST_LAG, 0)
             run(prepare_residual, step + 2)
             run(requantise, step - 4)
-            if step == 4 or step == 5:
+            if step in (4, 5):
                 quantise_rows(nc, w1_grouped, w1_codes, w1_scales, (step - 4) * BANK, BANK)
             run(bias_gelu_store, step - LAST_LAG, BANK)
             run(up_project, step - 5)
             if step == 1:
                 spread_b1()
                 turn_ln_vectors()
-            for block in {2: (0,), 3: (2,), 4: (4, 6)}.get(step, ()):
+            for block in {3: (0, 2), 4: (4, 6)}.get(step, ()):
                 flip_blocks(
                     nc, psum, identity, w1_words, w1_grouped_words, block, 2, nc.scalar.copy
                 )

@@ -26,7 +26,7 @@ FLOPS = 2 * TOKENS * K * D + 2 * TOKENS * K * F
 
 
 def flip_blocks(nc, psum, identity, rows, grouped, block, count, copy):
-    bank = psum.tile([P, count, 2, P], F32, tag="bank", bufs=4)
+    bank = psum.tile([P, count, 2, P], F32, tag="bank", bufs=5)
     for j in range(count):
         for u in range(2):
             nc.tensor.transpose(
@@ -162,7 +162,7 @@ def tile_block_pb_kernel(
             )
 
         def project(i):
-            product = psum.tile([P, D], F32, tag="mx", bufs=4)
+            product = psum.tile([P, D], F32, tag="mx", bufs=3)
             nc.tensor.matmul_mx(
                 out=product[:],
                 lhsT=o_codes[:, tokens(i)].bitcast(FP8X4),
@@ -219,7 +219,8 @@ def tile_block_pb_kernel(
             )
 
         def normalise(i):
-            nc.vector.tensor_scalar(
+            engine = nc.gpsimd if i == TILES - 1 else nc.vector
+            engine.tensor_scalar(
                 out=centred[:, i, :, :].rearrange("r (u e) p -> r u e p", e=2),
                 in0=x_glob[:, i, :].rearrange("r (u p e) -> r u e p", u=2, e=2),
                 scalar1=minus_mean[:, i : i + 1],
@@ -227,7 +228,7 @@ def tile_block_pb_kernel(
                 op0=ALU.add,
                 op1=ALU.mult,
             )
-            bank = psum.tile([P, PACK, P], F32, tag="bank", bufs=4)
+            bank = psum.tile([P, PACK, P], F32, tag="bank", bufs=5)
             for t in range(PACK):
                 nc.tensor.transpose(bank[:, t, :], centred[:, i, t, :], identity[:])
             flipped[i] = bank
@@ -253,7 +254,7 @@ def tile_block_pb_kernel(
 
         def up_project(i):
             for first in range(0, F, BANK):
-                up = psum.tile([P, BANK], F32, tag="mx", bufs=4)
+                up = psum.tile([P, BANK], F32, tag="mx", bufs=3)
                 nc.tensor.matmul_mx(
                     out=up[:],
                     lhsT=h_codes[:, tokens(i)].bitcast(FP8X4),
@@ -266,7 +267,7 @@ def tile_block_pb_kernel(
                 ups[i, first] = up
 
         def bias_gelu_store(i, first):
-            width = BANK // 2 if (i, first) == (TILES - 1, F - BANK) else BANK
+            width = BANK // 2 if i == TILES - 1 else BANK
             for start in range(first, first + BANK, width):
                 part = g[:, i, start : start + width]
                 nc.vector.tensor_tensor(
@@ -279,7 +280,7 @@ def tile_block_pb_kernel(
                 nc.sync.dma_start(out=g_out[tokens(i), start : start + width], in_=part)
 
         def spread_b1():
-            b1_bank = psum.tile([P, F], BF16, tag="bank", bufs=4)
+            b1_bank = psum.tile([P, F], BF16, tag="bank", bufs=5)
             for first in range(0, F, BANK):
                 nc.tensor.matmul(
                     out=b1_bank[:, first : first + BANK],
@@ -291,7 +292,7 @@ def tile_block_pb_kernel(
             nc.scalar.copy(out=bias_all[:, D:], in_=b1_bank[:])
 
         def turn_ln_vectors():
-            bank = psum.tile([P, P], F32, tag="bank", bufs=4)
+            bank = psum.tile([P, P], F32, tag="bank", bufs=5)
             nc.tensor.transpose(bank[:], ln_rows[:], identity[:])
             nc.scalar.copy(out=ln_words[:], in_=bank[:, :PACK])
             nc.gpsimd.tensor_copy(out=ln_affine[:], in_=ln_words[:].bitcast(BF16))
@@ -305,7 +306,7 @@ def tile_block_pb_kernel(
             flip_blocks(nc, psum, identity, wo_words, wo_grouped_words, block, 1, copy)
         flip_blocks(nc, psum, identity, o_words, o_grouped_words, 0, 2, nc.scalar.copy)
         quantise_rows(nc, wo_grouped, wo_codes, wo_scales, 0, D)
-        bo_bank = psum.tile([P, D], BF16, tag="bank", bufs=4)
+        bo_bank = psum.tile([P, D], BF16, tag="bank", bufs=5)
         nc.tensor.matmul(out=bo_bank[:], lhsT=ones[:], rhs=bo_rows[:], start=True, stop=True)
         nc.scalar.copy(out=bias_all[:, :D], in_=bo_bank[:])
         flip_blocks(nc, psum, identity, o_words, o_grouped_words, 2, 2, nc.scalar.copy)
@@ -317,22 +318,23 @@ def tile_block_pb_kernel(
         for step in range(TILES + LAST_LAG):
             run(project, step + 1)
             run(add_residual, step)
-            if step % 2 == 0 and step + 2 < TILES:
-                quantise_rows(nc, o_grouped, o_codes, o_scales, (step + 2) * P, 2 * P)
             run(scale_shift, step - 3)
             run(deviations, step)
             run(normalise, step - 2)
-            run(regroup, step - 4)
             run(bias_gelu_store, step - LAST_LAG, 0)
+            run(regroup, step - 4)
+            if step % 2 == 0 and step + 2 < TILES:
+                quantise_rows(nc, o_grouped, o_codes, o_scales, (step + 2) * P, 2 * P)
             run(prepare_residual, step + 2)
+            run(bias_gelu_store, step - LAST_LAG, BANK)
             run(requantise, step - 4)
             if step in (4, 5):
                 quantise_rows(nc, w1_grouped, w1_codes, w1_scales, (step - 4) * BANK, BANK)
-            run(bias_gelu_store, step - LAST_LAG, BANK)
             run(up_project, step - 5)
+            if step == 0:
+                turn_ln_vectors()
             if step == 1:
                 spread_b1()
-                turn_ln_vectors()
             for block in {3: (0, 2), 4: (4, 6)}.get(step, ()):
                 flip_blocks(
                     nc, psum, identity, w1_words, w1_grouped_words, block, 2, nc.scalar.copy

from contextlib import ExitStack

import concourse.mybir as mybir
from concourse.masks import make_identity

F32 = mybir.dt.float32
BF16 = mybir.dt.bfloat16
U32 = mybir.dt.uint32
U8 = mybir.dt.uint8
FP8X4 = mybir.dt.float8_e4m3fn_x4
ALU = mybir.AluOpType
ACT = mybir.ActivationFunctionType

P = 128
PACK = 4
K = P * PACK
TOKENS = 1024
TILES = TOKENS // P
D = 512
F = 1024
BANK = 512
EPS = 1e-5
LAST_LAG = 6

FLOPS = 2 * TOKENS * K * D + 2 * TOKENS * K * F


def flip_blocks(nc, psum, identity, rows, grouped, block, count, copy):
    bank = psum.tile([P, count, 2, P], F32, tag="bank", bufs=5)
    for j in range(count):
        for u in range(2):
            nc.tensor.transpose(
                bank[:, j, u, :], rows[:, block + j, u * P : (u + 1) * P], identity[:]
            )
    copy(
        out=grouped[:, block * P : (block + count) * P, :].rearrange(
            "p (j r) u -> p j r u", j=count
        ),
        in_=bank[:].rearrange("p j u r -> p j r u"),
    )


def quantise_rows(nc, grouped, codes, scales, first, count):
    nc.vector.quantize_mx(
        out=codes[:, first : first + count].bitcast(FP8X4),
        scales=scales[:, first : first + count],
        in_=grouped[:, first : first + count, :].rearrange("p r t -> p (r t)"),
    )


def tile_block_pb_kernel(
    tc, o_glob, x_loc, Wo_g, bo_g, ln3_w, ln3_b, W1, b1, out_0, out_1
):
    nc = tc.nc
    x_glob_out = out_0.flatten_outer_dims()
    g_out = out_1.flatten_outer_dims()

    with ExitStack() as stack:
        keep = stack.enter_context(tc.tile_pool(name="keep", bufs=1))
        psum = stack.enter_context(tc.psum_pool(name="psum", bufs=2))
        stack.enter_context(tc.manual_schedule())

        wo_rows = keep.tile([P, D // P, K], BF16)
        o_rows = keep.tile([P, TILES, K], BF16)
        x_rows = keep.tile([P, TILES, D], BF16)
        w1_rows = keep.tile([P, F // P, K], BF16)
        ln_rows = keep.tile([P, P], F32)
        ln_words = keep.tile([P, PACK], F32)
        ln_affine = keep.tile([P, 2 * PACK], F32)
        bo_rows = keep.tile([P, D], BF16)
        b1_rows = keep.tile([P, F], BF16)
        bias_all = keep.tile([P, D + F], BF16)
        ones = keep.tile([P, P], BF16)
        identity = keep.tile([P, P], F32)
        minus_half = keep.tile([P, 1], F32)
        table_in = keep.tile([P, 1], F32)
        table_out = keep.tile([P, 1], F32)

        wo_grouped = keep.tile([P, D, PACK], BF16, align_bytes=64)
        wo_codes = keep.tile([P, D], U32, align_bytes=64)
        wo_scales = keep.tile([P, D], U8, align_bytes=64)
        o_grouped = keep.tile([P, TOKENS, PACK], BF16, align_bytes=64)
        o_codes = keep.tile([P, TOKENS], U32, align_bytes=64)
        o_scales = keep.tile([P, TOKENS], U8, align_bytes=64)
        w1_grouped = keep.tile([P, F, PACK], BF16, align_bytes=64)
        w1_codes = keep.tile([P, F], U32, align_bytes=64)
        w1_scales = keep.tile([P, F], U8, align_bytes=64)
        h_grouped = keep.tile([P, TOKENS, PACK], BF16, align_bytes=64)
        h_codes = keep.tile([P, TOKENS], U32, align_bytes=64)
        h_scales = keep.tile([P, TOKENS], U8, align_bytes=64)

        x_glob = keep.tile([P, TILES, D], F32)
        squares = keep.tile([P, TILES, D], BF16)
        centred = keep.tile([P, TILES, PACK, P], F32)
        h_planes = keep.tile([P, TILES, PACK, P], BF16)
        g = keep.tile([P, TILES, F], F32)
        row_sum = keep.tile([P, TILES], F32)
        minus_mean = keep.tile([P, TILES], F32)
        square_sum = keep.tile([P, TILES], F32)
        var_eps = keep.tile([P, TILES], F32)
        inv_std = keep.tile([P, TILES], F32)

        products = {}
        flipped = {}
        ups = {}

        nc.vector.memset(bo_rows[:], 0.0)
        nc.vector.memset(ln_rows[:], 0.0)
        nc.vector.memset(b1_rows[:], 0.0)
        nc.vector.memset(ones[:], 1.0)
        nc.vector.memset(minus_half[:], -0.5)
        nc.vector.memset(table_in[:], 0.0)
        make_identity(nc, identity[:])
        nc.scalar.activation(out=table_out[:], in_=table_in[:], func=ACT.Gelu)

        o_tiles = o_glob.rearrange("b n (h s) d -> b h s n d", s=P)
        x_tiles = x_loc.flatten_outer_dims().rearrange("(i r) d -> r i d", r=P)
        wo_blocks = Wo_g.rearrange("(c r) k -> r c k", r=P)
        w1_blocks = W1.rearrange("(c r) k -> r c k", r=P)

        def load_o_pair(first):
            for i in (first, first + 1):
                nc.sync.dma_start(
                    out=o_rows[:, i, :].rearrange("s (n d) -> s n d", d=P),
                    in_=o_tiles[i // 2, i % 2],
                )

        def load_x_pair(first):
            nc.sync.dma_start(
                out=x_rows[:, first : first + 2, :], in_=x_tiles[:, first : first + 2, :]
            )

        nc.gpsimd.dma_start(
            out=ln_rows[0:2, :].bitcast(BF16), in_=ln3_w.rearrange("(u w) -> u w", u=2)
        )
        nc.gpsimd.dma_start(
            out=ln_rows[2:4, :].bitcast(BF16), in_=ln3_b.rearrange("(u w) -> u w", u=2)
        )
        nc.gpsimd.dma_start(out=b1_rows[0:1, :], in_=b1.unsqueeze(0))
        nc.sync.dma_start(out=wo_rows[:, :2, :], in_=wo_blocks[:, :2, :])
        nc.sync.dma_start(out=wo_rows[:, 2:, :], in_=wo_blocks[:, 2:, :])
        nc.sync.dma_start(out=bo_rows[0:1, :], in_=bo_g.unsqueeze(0))
        for pair in range(0, TILES, 2):
            load_o_pair(pair)
            load_x_pair(pair)
        nc.sync.dma_start(out=w1_rows[:, :4, :], in_=w1_blocks[:, :4, :])
        nc.sync.dma_start(out=w1_rows[:, 4:, :], in_=w1_blocks[:, 4:, :])

        o_words = o_rows[:].bitcast(F32)
        o_grouped_words = o_grouped[:].bitcast(F32)
        wo_words = wo_rows[:].bitcast(F32)
        wo_grouped_words = wo_grouped[:].bitcast(F32)
        w1_words = w1_rows[:].bitcast(F32)
        w1_grouped_words = w1_grouped[:].bitcast(F32)

        def tokens(i):
            return slice(i * P, (i + 1) * P)

        def prepare_residual(i):
            nc.vector.tensor_tensor(
                out=x_glob[:, i, :], in0=x_rows[:, i, :], in1=bias_all[:, :D], op=ALU.add
            )

        def project(i):
            product = psum.tile([P, D], F32, tag="mx", bufs=3)
            nc.tensor.matmul_mx(
                out=product[:],
                lhsT=o_codes[:, tokens(i)].bitcast(FP8X4),
                lhsT_scale=o_scales[:, tokens(i)],
                rhs=wo_codes[:].bitcast(FP8X4),
                rhs_scale=wo_scales[:],
                start=True,
                stop=True,
            )
            products[i] = product

        def add_residual(i):
            nc.vector.scalar_tensor_tensor(
                out=x_glob[:, i, :],
                in0=products[i][:],
                scalar=0.0,
                in1=x_glob[:, i, :],
                op0=ALU.add,
                op1=ALU.add,
                accum_out=row_sum[:, i : i + 1],
            )
            nc.sync.dma_start(out=x_glob_out[tokens(i), :], in_=x_glob[:, i, :])
            nc.gpsimd.tensor_scalar(
                out=minus_mean[:, i : i + 1],
                in0=row_sum[:, i : i + 1],
                scalar1=-1.0 / D,
                scalar2=0.0,
                op0=ALU.mult,
                op1=ALU.add,
            )

        def deviations(i):
            nc.scalar.activation(
                out=squares[:, i, :],
                in_=x_glob[:, i, :],
                func=ACT.Square,
                bias=row_sum[:, i : i + 1],
                scale=-1.0 * D,
                accum_out=square_sum[:, i : i + 1],
            )
            nc.gpsimd.tensor_scalar(
                out=var_eps[:, i : i + 1],
                in0=square_sum[:, i : i + 1],
                scalar1=1.0 / (D * D * D),
                scalar2=EPS,
                op0=ALU.mult,
                op1=ALU.add,
            )
            nc.gpsimd.tensor_tensor(
                out=inv_std[:, i : i + 1],
                in0=var_eps[:, i : i + 1],
                in1=minus_half[:],
                op=ALU.pow,
            )

        def normalise(i):
            engine = nc.gpsimd if i == TILES - 1 else nc.vector
            engine.tensor_scalar(
                out=centred[:, i, :, :].rearrange("r (u e) p -> r u e p", e=2),
                in0=x_glob[:, i, :].rearrange("r (u p e) -> r u e p", u=2, e=2),
                scalar1=minus_mean[:, i : i + 1],
                scalar2=inv_std[:, i : i + 1],
                op0=ALU.add,
                op1=ALU.mult,
            )
            bank = psum.tile([P, PACK, P], F32, tag="bank", bufs=5)
            for t in range(PACK):
                nc.tensor.transpose(bank[:, t, :], centred[:, i, t, :], identity[:])
            flipped[i] = bank

        def scale_shift(i):
            for t in range(PACK):
                nc.scalar.activation(
                    out=h_planes[:, i, t, :],
                    in_=flipped[i][:, t, :],
                    func=ACT.Identity,
                    scale=ln_affine[:, t : t + 1],
                    bias=ln_affine[:, PACK + t : PACK + t + 1],
                )

        def regroup(i):
            nc.vector.tensor_copy(
                out=h_grouped[:, tokens(i), :].rearrange("p (c i) t -> p c t i", i=4),
                in_=h_planes[:, i, :, :].rearrange("p t (c i) -> p c t i", i=4),
            )

        def requantise(i):
            quantise_rows(nc, h_grouped, h_codes, h_scales, i * P, P)

        def up_project(i):
            for first in range(0, F, BANK):
                up = psum.tile([P, BANK], F32, tag="mx", bufs=3)
                nc.tensor.matmul_mx(
                    out=up[:],
                    lhsT=h_codes[:, tokens(i)].bitcast(FP8X4),
                    lhsT_scale=h_scales[:, tokens(i)],
                    rhs=w1_codes[:, first : first + BANK].bitcast(FP8X4),
                    rhs_scale=w1_scales[:, first : first + BANK],
                    start=True,
                    stop=True,
                )
                ups[i, first] = up

        def bias_gelu_store(i, first):
            width = BANK // 2 if i == TILES - 1 else BANK
            for start in range(first, first + BANK, width):
                part = g[:, i, start : start + width]
                nc.vector.tensor_tensor(
                    out=part,
                    in0=ups[i, first][:, start - first : start - first + width],
                    in1=bias_all[:, D + start : D + start + width],
                    op=ALU.add,
                )
                nc.scalar.activation(out=part, in_=part, func=ACT.Gelu)
                nc.sync.dma_start(out=g_out[tokens(i), start : start + width], in_=part)

        def spread_b1():
            b1_bank = psum.tile([P, F], BF16, tag="bank", bufs=5)
            for first in range(0, F, BANK):
                nc.tensor.matmul(
                    out=b1_bank[:, first : first + BANK],
                    lhsT=ones[:],
                    rhs=b1_rows[:, first : first + BANK],
                    start=True,
                    stop=True,
                )
            nc.scalar.copy(out=bias_all[:, D:], in_=b1_bank[:])

        def turn_ln_vectors():
            bank = psum.tile([P, P], F32, tag="bank", bufs=5)
            nc.tensor.transpose(bank[:], ln_rows[:], identity[:])
            nc.scalar.copy(out=ln_words[:], in_=bank[:, :PACK])
            nc.gpsimd.tensor_copy(out=ln_affine[:], in_=ln_words[:].bitcast(BF16))

        def run(stage, i, *rest):
            if 0 <= i < TILES:
                stage(i, *rest)

        for block in range(D // P):
            copy = nc.vector.tensor_copy if block % 2 else nc.scalar.copy
            flip_blocks(nc, psum, identity, wo_words, wo_grouped_words, block, 1, copy)
        flip_blocks(nc, psum, identity, o_words, o_grouped_words, 0, 2, nc.scalar.copy)
        quantise_rows(nc, wo_grouped, wo_codes, wo_scales, 0, D)
        bo_bank = psum.tile([P, D], BF16, tag="bank", bufs=5)
        nc.tensor.matmul(out=bo_bank[:], lhsT=ones[:], rhs=bo_rows[:], start=True, stop=True)
        nc.scalar.copy(out=bias_all[:, :D], in_=bo_bank[:])
        flip_blocks(nc, psum, identity, o_words, o_grouped_words, 2, 2, nc.scalar.copy)
        quantise_rows(nc, o_grouped, o_codes, o_scales, 0, 2 * P)
        prepare_residual(0)
        prepare_residual(1)
        project(0)

        for step in range(TILES + LAST_LAG):
            run(project, step + 1)
            run(add_residual, step)
            run(scale_shift, step - 3)
            run(deviations, step)
            run(normalise, step - 2)
            run(bias_gelu_store, step - LAST_LAG, 0)
            run(regroup, step - 4)
            if step % 2 == 0 and step + 2 < TILES:
                quantise_rows(nc, o_grouped, o_codes, o_scales, (step + 2) * P, 2 * P)
            run(prepare_residual, step + 2)
            run(bias_gelu_store, step - LAST_LAG, BANK)
            run(requantise, step - 4)
            if step in (4, 5):
                quantise_rows(nc, w1_grouped, w1_codes, w1_scales, (step - 4) * BANK, BANK)
            run(up_project, step - 5)
            if step == 0:
                turn_ln_vectors()
            if step == 1:
                spread_b1()
            for block in {3: (0, 2), 4: (4, 6)}.get(step, ()):
                flip_blocks(
                    nc, psum, identity, w1_words, w1_grouped_words, block, 2, nc.scalar.copy
                )
            if step % 2 == 0 and step + 4 < TILES:
                flip_blocks(
                    nc, psum, identity, o_words, o_grouped_words, step + 4, 2, nc.scalar.copy
                )
